import numpy as np
import ml_dtypes


def mxq(x, axis, fmt="e4m3"):
    dtype, down = {"e4m3": (ml_dtypes.float8_e4m3fn, 7), "e5m2": (ml_dtypes.float8_e5m2, 14)}[fmt]
    v = np.moveaxis(np.asarray(x, np.float32).astype(ml_dtypes.bfloat16).astype(np.float64), axis, -1)
    blocks = v.reshape(v.shape[:-1] + (-1, 32))
    amax = np.abs(blocks).max(-1, keepdims=True)
    byte = np.maximum(np.where(amax > 0, np.frexp(amax)[1] - 1 + 127, 0) - down, 1)
    scale = np.exp2(byte - 127.0)
    codes = (blocks / scale).astype(np.float32).astype(dtype).astype(np.float64)
    return np.moveaxis((codes * scale).reshape(v.shape), -1, axis)


WIDE = False


def mx_kscale(k):
    if not WIDE:
        return np.ones(k)
    levels = np.array([10, -10, 5, -5, 0])
    a = np.random.permutation(np.resize(levels, k // 512 * 4)).reshape(k // 512, 4)
    idx = np.arange(k)
    return np.exp2(a[idx // 512, idx % 128 // 32])


BF16 = ml_dtypes.bfloat16


def bf(x):
    return np.asarray(x, np.float32).astype(BF16)


def f64(x):
    return np.asarray(x).astype(np.float64)


E2M1 = np.array([0.0, 0.5, 1.0, 1.5, 2.0, 3.0, 4.0, 6.0, -0.0, -0.5, -1.0, -1.5, -2.0, -3.0, -4.0, -6.0])


def pack_weight(w, fmt):
    k, n = w.shape
    w = f64(bf(w)).reshape(k // 32, 32, n)
    amax = np.abs(w).max(1)
    if fmt == "e4m3":
        byte = np.frexp(amax)[1] - 1 + 127 - 7
    else:
        mant, ex = np.frexp(amax / 6.0)
        byte = np.where(mant > 0.5, ex, ex - 1) + 127
    byte = np.clip(np.where(amax > 0, byte, 1), 1, 254)
    scaled = (w * np.exp2(127.0 - byte)[:, None, :]).reshape(k, n).astype(np.float32)
    by_word = np.ascontiguousarray(scaled.reshape(k // 512, 128, 4, n).transpose(0, 1, 3, 2))
    if fmt == "e4m3":
        words = by_word.astype(ml_dtypes.float8_e4m3fn).view(np.uint8)
    else:
        c = by_word.astype(ml_dtypes.float4_e2m1fn).view(np.uint8) & 0xF
        words = c[..., 0::2] | (c[..., 1::2] << 4)
    return np.ascontiguousarray(words), np.ascontiguousarray(byte.astype(np.uint8).reshape(k // 512, 16, n))


def unpack_weight(words, scales, fmt):
    g, p, n, _ = words.shape
    if fmt == "e4m3":
        vals = np.ascontiguousarray(words).view(ml_dtypes.float8_e4m3fn).astype(np.float64)
    else:
        nib = np.empty((g, p, n, 4), np.uint8)
        nib[..., 0::2] = words & 0xF
        nib[..., 1::2] = words >> 4
        vals = E2M1[nib]
    vals = vals * np.repeat(np.exp2(scales.astype(np.float64) - 127.0), 8, axis=1)[..., None]
    return vals.transpose(0, 1, 3, 2).reshape(g * 512, n)

def pack4(w):
    words, scales = pack_weight(w, "e2m1")
    return words.reshape(words.shape[0], 128, -1), scales


def unpack4(words, scales):
    return unpack_weight(words.reshape(words.shape[0], 128, -1, 2), scales, "e2m1")


B, H, P, D, NF, DO, G = 2, 4, 16, 512, 8, 512, 5
N = D * H * P


def setup_inputs():
    s = mx_kscale(D)
    x = bf(np.random.standard_normal((B, H, P, D)) * s)
    lin_w = np.random.standard_normal((G * D, D)) * 0.3 / np.sqrt(D) / s
    words, scales = pack4(lin_w.T)
    return {
        "x": x,
        "lin_w_words": words,
        "lin_w_scales": scales,
        "lin_b": bf(np.random.standard_normal(G * D) * 0.1),
        "grid": bf(np.arange(NF)[None, :] + 1.0 + 0.1 * np.random.standard_normal((G, NF))),
        "coef": bf(np.random.standard_normal((N, NF, G)) * 0.5),
        "shift": bf(np.random.standard_normal((1, H, G, P, D)) * 0.5),
    }


def reference(x, lin_w_words, lin_w_scales, lin_b, grid, coef, shift):
    xl = (mxq(f64(x), 3, "e4m3") @ unpack4(lin_w_words, lin_w_scales)) + f64(lin_b)
    xl = xl.reshape(B, G, N)
    sn = np.sin(f64(grid)[None, :, :, None] * xl[:, :, None, :])
    f = sn * f64(coef).transpose(2, 1, 0)[None]
    return f.reshape(B, H, G, NF, P, D).sum(axis=3) + f64(shift)

@@ -1,0 +1,189 @@
+import math
+from contextlib import ExitStack
+
+import concourse.mybir as mybir
+from concourse.masks import make_identity
+
+F32 = mybir.dt.float32
+BF16 = mybir.dt.bfloat16
+I32 = mybir.dt.int32
+U32 = mybir.dt.uint32
+U8 = mybir.dt.uint8
+FP8X4 = mybir.dt.float8_e4m3fn_x4
+FP4X4 = mybir.dt.float4_e2m1fn_x4
+ALU = mybir.AluOpType
+ACT = mybir.ActivationFunctionType
+
+P = 128
+ROWS = 128
+K = 512
+GROUPS = 5
+FREQS = 8
+COLS = GROUPS * K
+CHUNKS = 5
+QUARTERS = 4
+HALF_FREQS = 4
+TERMS = 4
+ROUND_MAGIC = 12582912.0
+
+FLOPS = 2 * ROWS * K * COLS
+
+
+def tile_ka_attention_heads_mod_pa_s_kernel(
+    tc, x, lin_w_words, lin_w_scales, lin_b, grid, coef, shift, out
+):
+    nc = tc.nc
+    with ExitStack() as stack:
+        keep = stack.enter_context(tc.tile_pool(name="keep", bufs=1))
+        work = stack.enter_context(tc.tile_pool(name="work", bufs=3))
+        psum = stack.enter_context(tc.psum_pool(name="psum", bufs=8))
+
+        x_sb = keep.tile([P, K], BF16, name="x_sb")
+        nc.sync.dma_start(out=x_sb[:], in_=x.flatten_outer_dims())
+
+        w_planes = keep.tile([P, COLS], U8, name="w_planes", align_bytes=64)
+        nc.vector.memset(w_planes[:].bitcast(I32), 0)
+        scale_rows = lin_w_scales[0].rearrange("(q r) n -> r q n", r=4)
+        for r in range(4):
+            nc.sync.dma_start(
+                out=w_planes[r:P:32, :].bitcast(I32), in_=scale_rows[r].bitcast(I32)
+            )
+        w_words = keep.tile([P, 2 * COLS], U8, name="w_words", align_bytes=64)
+        nc.sync.dma_start(out=w_words[:].bitcast(I32), in_=lin_w_words[0].bitcast(I32))
+
+        bias_rows = keep.tile([P, P], BF16, name="bias_rows")
+        nc.vector.memset(bias_rows[:], 0.0)
+        nc.scalar.dma_start(
+            out=bias_rows[0 : COLS // P, :], in_=lin_b.rearrange("(r c) -> r c", c=P)
+        )
+        grid_all = keep.tile([P, GROUPS * FREQS], BF16, name="grid_all")
+        nc.scalar.dma_start(
+            out=grid_all[:], in_=grid.rearrange("g f -> (g f)").partition_broadcast(P)
+        )
+
+        coef_sb = keep.tile([P, 2, P * FREQS * GROUPS], BF16, name="coef_sb")
+        coef_halves = coef.rearrange("(a p l) m j -> a p (l m j)", a=2, p=P)
+        for a in range(2):
+            nc.sync.dma_start(out=coef_sb[:, a, :], in_=coef_halves[a])
+
+        shift_sb = keep.tile([P, 4 * GROUPS, P], BF16, name="shift_sb")
+        shift_view = shift[0].rearrange("h g p (d l) -> (p d) (h g) l", d=QUARTERS)
+        for b in range(2):
+            nc.sync.dma_start(out=shift_sb[64 * b : 64 * (b + 1)], in_=shift_view)
+
+        ident_f32 = keep.tile([P, P], F32, name="ident_f32")
+        make_identity(nc, ident_f32[:])
+        ident_bf16 = keep.tile([P, P], BF16, name="ident_bf16")
+        make_identity(nc, ident_bf16[:])
+
+        warm_in = keep.tile([P, 1], F32, name="warm_in")
+        warm_out = keep.tile([P, 1], F32, name="warm_out")
+        nc.vector.memset(warm_in[:], 0.0)
+        nc.scalar.activation(out=warm_out[:], in_=warm_in[:], func=ACT.Sin)
+
+        x_words = x_sb[:].bitcast(F32)
+        x_t = psum.tile([P, 2, ROWS], F32, name="x_t", tag="bank")
+        for u in range(2):
+            nc.tensor.transpose(x_t[:, u, :], x_words[:, u : K // 2 : 2], ident_f32[:])
+        grouped = keep.tile([P, ROWS, 4], BF16, name="grouped", align_bytes=64)
+        nc.vector.tensor_copy(
+            out=grouped[:].rearrange("p r t -> p (r t)").bitcast(F32).rearrange("p (r u) -> p r u", u=2),
+            in_=x_t[:].rearrange("p u r -> p r u"),
+        )
+        x_codes = keep.tile([P, ROWS], U32, name="x_codes", align_bytes=64)
+        x_scales = keep.tile([P, ROWS], U8, name="x_scales", align_bytes=64)
+        nc.vector.quantize_mx(
+            out=x_codes[:].bitcast(FP8X4),
+            scales=x_scales[:],
+            in_=grouped[:].rearrange("p r t -> p (r t)"),
+        )
+
+        bias_ps = psum.tile([P, P], BF16, name="bias_ps", tag="bank")
+        nc.tensor.transpose(bias_ps[:], bias_rows[:], ident_bf16[:])
+        bias_t = keep.tile([P, COLS // P], F32, name="bias_t")
+        nc.vector.tensor_copy(out=bias_t[:], in_=bias_ps[:, 0 : COLS // P])
+        turns = keep.tile([P, GROUPS * FREQS], F32, name="turns")
+        nc.vector.tensor_scalar(
+            out=turns[:], in0=grid_all[:], scalar1=1.0 / (2.0 * math.pi), scalar2=None, op0=ALU.mult
+        )
+
+        xl = keep.tile([P, ROWS, CHUNKS, QUARTERS], F32, name="xl")
+        for cc in range(CHUNKS):
+            acc = psum.tile([P, QUARTERS, ROWS], F32, name="acc", tag="bank")
+            for dq in range(QUARTERS):
+                block = cc * QUARTERS + dq
+                nc.tensor.matmul_mx(
+                    out=acc[:, dq, :],
+                    lhsT=w_words[:, 2 * P * block : 2 * P * (block + 1)].bitcast(FP4X4),
+                    lhsT_scale=w_planes[:, P * block : P * (block + 1)],
+                    rhs=x_codes[:].bitcast(FP8X4),
+                    rhs_scale=x_scales[:],
+                    start=True,
+                    stop=True,
+                )
+            nc.vector.tensor_tensor(
+                out=xl[:, :, cc, :],
+                in0=acc[:].rearrange("p d n -> p n d"),
+                in1=bias_t[:, cc * QUARTERS : (cc + 1) * QUARTERS].unsqueeze(1).to_broadcast([P, ROWS, QUARTERS]),
+                op=ALU.add,
+            )
+        xl_groups = xl[:].rearrange("p n c d -> p (n c d)").rearrange(
+            "p (b j a f) -> p j a b f", b=2, j=GROUPS, a=TERMS
+        )
+        coef_cols = coef_sb[:].rearrange("p a (l m j) -> p a l m j", m=FREQS, j=GROUPS)
+        out_views = [out[b].rearrange("h g p (d l) -> (p d) (h g) l", d=QUARTERS) for b in range(2)]
+
+        for j in range(GROUPS):
+            summed = psum.tile([P, 4, P], F32, name="summed", tag="bank")
+            for h in range(2):
+                coef_t = psum.tile([P, HALF_FREQS * TERMS, 64], BF16, name="coef_t", tag="bank")
+                for mi in range(HALF_FREQS):
+                    for a in range(2):
+                        nc.tensor.transpose(
+                            coef_t[:, mi * TERMS + 2 * a : mi * TERMS + 2 * a + 2, :].rearrange("p g f -> p (g f)"),
+                            coef_cols[:, a, :, h * HALF_FREQS + mi, j],
+                            ident_bf16[:],
+                        )
+                angle = work.tile([P, HALF_FREQS * TERMS, 2, 64], F32, name="angle")
+                for mi in range(HALF_FREQS):
+                    jm = j * FREQS + h * HALF_FREQS + mi
+                    nc.scalar.activation(
+                        out=angle[:, mi * TERMS : (mi + 1) * TERMS],
+                        in_=xl_groups[:, j],
+                        func=ACT.Copy,
+                        scale=turns[:, jm : jm + 1],
+                    )
+                whole = work.tile([P, HALF_FREQS * TERMS, 2, 64], F32, name="whole")
+                nc.vector.tensor_scalar(
+                    out=whole[:], in0=angle[:], scalar1=ROUND_MAGIC, scalar2=ROUND_MAGIC,
+                    op0=ALU.add, op1=ALU.subtract,
+                )
+                frac = work.tile([P, HALF_FREQS * TERMS, 2, 64], F32, name="frac")
+                nc.vector.tensor_tensor(out=frac[:], in0=angle[:], in1=whole[:], op=ALU.subtract)
+                sine = work.tile([P, HALF_FREQS * TERMS, 2, 64], F32, name="sine")
+                nc.scalar.activation(out=sine[:], in_=frac[:], func=ACT.Sin, scale=2.0 * math.pi)
+                prod = work.tile([P, HALF_FREQS * TERMS, 2, 64], F32, name="prod")
+                nc.vector.tensor_tensor(
+                    out=prod[:],
+                    in0=sine[:],
+                    in1=coef_t[:].unsqueeze(2).to_broadcast([P, HALF_FREQS * TERMS, 2, 64]),
+                    op=ALU.mult,
+                )
+                for pair in range(2):
+                    for term in range(2 * TERMS):
+                        nc.tensor.matmul(
+                            out=summed[:, 2 * h + pair, :],
+                            lhsT=prod[:, pair * 2 * TERMS + term].rearrange("p b f -> p (b f)"),
+                            rhs=ident_f32[:],
+                            start=(term == 0),
+                            stop=(term == 2 * TERMS - 1),
+                            is_transpose=True,
+                        )
+            result = work.tile([P, 4, P], F32, name="result")
+            nc.vector.tensor_tensor(
+                out=result[:], in0=summed[:], in1=shift_sb[:, 4 * j : 4 * (j + 1), :], op=ALU.add
+            )
+            for b in range(2):
+                nc.sync.dma_start(
+                    out=out_views[b][:, 4 * j : 4 * (j + 1), :], in_=result[64 * b : 64 * (b + 1)]
+                )

@@ -25,6 +25,7 @@ QUARTERS = 4
 HALF_FREQS = 4
 TERMS = 4
 ROUND_MAGIC = 12582912.0
+POOL_FREQS = 2
 
 FLOPS = 2 * ROWS * K * COLS
 
@@ -153,15 +154,32 @@ def tile_ka_attention_heads_mod_pa_s_kernel(
                         func=ACT.Copy,
                         scale=turns[:, jm : jm + 1],
                     )
-                whole = work.tile([P, HALF_FREQS * TERMS, 2, 64], F32, name="whole")
+                lifted = work.tile([P, HALF_FREQS * TERMS, 2, 64], F32, name="lifted")
+                for mi in range(POOL_FREQS):
+                    jm = j * FREQS + h * HALF_FREQS + mi
+                    nc.gpsimd.tensor_scalar(
+                        out=lifted[:, mi * TERMS : (mi + 1) * TERMS],
+                        in0=xl_groups[:, j],
+                        scalar1=turns[:, jm : jm + 1],
+                        scalar2=ROUND_MAGIC,
+                        op0=ALU.mult,
+                        op1=ALU.add,
+                    )
                 nc.vector.tensor_scalar(
-                    out=whole[:], in0=angle[:], scalar1=ROUND_MAGIC, scalar2=ROUND_MAGIC,
-                    op0=ALU.add, op1=ALU.subtract,
+                    out=lifted[:, POOL_FREQS * TERMS :], in0=angle[:, POOL_FREQS * TERMS :],
+                    scalar1=ROUND_MAGIC, scalar2=None, op0=ALU.add,
                 )
-                frac = work.tile([P, HALF_FREQS * TERMS, 2, 64], F32, name="frac")
-                nc.vector.tensor_tensor(out=frac[:], in0=angle[:], in1=whole[:], op=ALU.subtract)
+                minus_frac = work.tile([P, HALF_FREQS * TERMS, 2, 64], F32, name="minus_frac")
+                nc.vector.scalar_tensor_tensor(
+                    out=minus_frac[:].rearrange("p g b f -> p (g b f)"),
+                    in0=lifted[:].rearrange("p g b f -> p (g b f)"),
+                    scalar=ROUND_MAGIC,
+                    in1=angle[:].rearrange("p g b f -> p (g b f)"),
+                    op0=ALU.subtract,
+                    op1=ALU.subtract,
+                )
                 sine = work.tile([P, HALF_FREQS * TERMS, 2, 64], F32, name="sine")
-                nc.scalar.activation(out=sine[:], in_=frac[:], func=ACT.Sin, scale=2.0 * math.pi)
+                nc.scalar.activation(out=sine[:], in_=minus_frac[:], func=ACT.Sin, scale=-2.0 * math.pi)
                 prod = work.tile([P, HALF_FREQS * TERMS, 2, 64], F32, name="prod")
                 nc.vector.tensor_tensor(
                     out=prod[:],

@@ -22,10 +22,10 @@ FREQS = 8
 COLS = GROUPS * K
 CHUNKS = 5
 QUARTERS = 4
-HALF_FREQS = 4
+PAIRS = FREQS // 2
+UNITS = GROUPS * PAIRS
 TERMS = 4
 ROUND_MAGIC = 12582912.0
-POOL_FREQS = 2
 
 FLOPS = 2 * ROWS * K * COLS
 
@@ -34,10 +34,14 @@ def tile_ka_attention_heads_mod_pa_s_kernel(
     tc, x, lin_w_words, lin_w_scales, lin_b, grid, coef, shift, out
 ):
     nc = tc.nc
+    unit_shape = [P, 2 * TERMS, 2, 64]
     with ExitStack() as stack:
         keep = stack.enter_context(tc.tile_pool(name="keep", bufs=1))
         work = stack.enter_context(tc.tile_pool(name="work", bufs=3))
-        psum = stack.enter_context(tc.psum_pool(name="psum", bufs=8))
+        psum_setup = stack.enter_context(tc.psum_pool(name="psum_setup", bufs=3))
+        psum_coef = stack.enter_context(tc.psum_pool(name="psum_coef", bufs=3))
+        psum_sum = stack.enter_context(tc.psum_pool(name="psum_sum", bufs=2))
+        stack.enter_context(tc.manual_schedule())
 
         x_sb = keep.tile([P, K], BF16, name="x_sb")
         nc.sync.dma_start(out=x_sb[:], in_=x.flatten_outer_dims())
@@ -67,7 +71,7 @@ def tile_ka_attention_heads_mod_pa_s_kernel(
         for a in range(2):
             nc.sync.dma_start(out=coef_sb[:, a, :], in_=coef_halves[a])
 
-        shift_sb = keep.tile([P, 4 * GROUPS, P], BF16, name="shift_sb")
+        shift_sb = keep.tile([P, PAIRS * GROUPS, P], BF16, name="shift_sb")
         shift_view = shift[0].rearrange("h g p (d l) -> (p d) (h g) l", d=QUARTERS)
         for b in range(2):
             nc.sync.dma_start(out=shift_sb[64 * b : 64 * (b + 1)], in_=shift_view)
@@ -83,7 +87,7 @@ def tile_ka_attention_heads_mod_pa_s_kernel(
         nc.scalar.activation(out=warm_out[:], in_=warm_in[:], func=ACT.Sin)
 
         x_words = x_sb[:].bitcast(F32)
-        x_t = psum.tile([P, 2, ROWS], F32, name="x_t", tag="bank")
+        x_t = psum_setup.tile([P, 2, ROWS], F32, name="x_t", tag="setup")
         for u in range(2):
             nc.tensor.transpose(x_t[:, u, :], x_words[:, u : K // 2 : 2], ident_f32[:])
         grouped = keep.tile([P, ROWS, 4], BF16, name="grouped", align_bytes=64)
@@ -99,18 +103,19 @@ def tile_ka_attention_heads_mod_pa_s_kernel(
             in_=grouped[:].rearrange("p r t -> p (r t)"),
         )
 
-        bias_ps = psum.tile([P, P], BF16, name="bias_ps", tag="bank")
+        bias_ps = psum_setup.tile([P, P], BF16, name="bias_ps", tag="setup")
         nc.tensor.transpose(bias_ps[:], bias_rows[:], ident_bf16[:])
         bias_t = keep.tile([P, COLS // P], F32, name="bias_t")
         nc.vector.tensor_copy(out=bias_t[:], in_=bias_ps[:, 0 : COLS // P])
         turns = keep.tile([P, GROUPS * FREQS], F32, name="turns")
-        nc.vector.tensor_scalar(
-            out=turns[:], in0=grid_all[:], scalar1=1.0 / (2.0 * math.pi), scalar2=None, op0=ALU.mult
+        nc.gpsimd.tensor_scalar(
+            out=turns[:], in0=grid_all[:], scalar1=1.0 / (2.0 * math.pi), scalar2=0.0,
+            op0=ALU.mult, op1=ALU.add,
         )
 
         xl = keep.tile([P, ROWS, CHUNKS, QUARTERS], F32, name="xl")
         for cc in range(CHUNKS):
-            acc = psum.tile([P, QUARTERS, ROWS], F32, name="acc", tag="bank")
+            acc = psum_setup.tile([P, QUARTERS, ROWS], F32, name="acc", tag="setup")
             for dq in range(QUARTERS):
                 block = cc * QUARTERS + dq
                 nc.tensor.matmul_mx(
@@ -134,74 +139,101 @@ def tile_ka_attention_heads_mod_pa_s_kernel(
         coef_cols = coef_sb[:].rearrange("p a (l m j) -> p a l m j", m=FREQS, j=GROUPS)
         out_views = [out[b].rearrange("h g p (d l) -> (p d) (h g) l", d=QUARTERS) for b in range(2)]
 
-        for j in range(GROUPS):
-            summed = psum.tile([P, 4, P], F32, name="summed", tag="bank")
-            for h in range(2):
-                coef_t = psum.tile([P, HALF_FREQS * TERMS, 64], BF16, name="coef_t", tag="bank")
-                for mi in range(HALF_FREQS):
-                    for a in range(2):
-                        nc.tensor.transpose(
-                            coef_t[:, mi * TERMS + 2 * a : mi * TERMS + 2 * a + 2, :].rearrange("p g f -> p (g f)"),
-                            coef_cols[:, a, :, h * HALF_FREQS + mi, j],
-                            ident_bf16[:],
-                        )
-                angle = work.tile([P, HALF_FREQS * TERMS, 2, 64], F32, name="angle")
-                for mi in range(HALF_FREQS):
-                    jm = j * FREQS + h * HALF_FREQS + mi
-                    nc.scalar.activation(
-                        out=angle[:, mi * TERMS : (mi + 1) * TERMS],
-                        in_=xl_groups[:, j],
-                        func=ACT.Copy,
-                        scale=turns[:, jm : jm + 1],
+        angle_of = {}
+        whole_of = {}
+        coef_t_of = {}
+        sine_of = {}
+        summed_of = {}
+
+        def coefficients(u):
+            j, m2 = divmod(u, PAIRS)
+            coef_t = psum_coef.tile([P, 2 * TERMS, 64], BF16, name="coef_t")
+            for e in range(2):
+                for a in range(2):
+                    nc.tensor.transpose(
+                        coef_t[:, e * TERMS + 2 * a : e * TERMS + 2 * a + 2, :].rearrange("p g f -> p (g f)"),
+                        coef_cols[:, a, :, 2 * m2 + e, j],
+                        ident_bf16[:],
                     )
-                lifted = work.tile([P, HALF_FREQS * TERMS, 2, 64], F32, name="lifted")
-                for mi in range(POOL_FREQS):
-                    jm = j * FREQS + h * HALF_FREQS + mi
-                    nc.gpsimd.tensor_scalar(
-                        out=lifted[:, mi * TERMS : (mi + 1) * TERMS],
-                        in0=xl_groups[:, j],
-                        scalar1=turns[:, jm : jm + 1],
-                        scalar2=ROUND_MAGIC,
-                        op0=ALU.mult,
-                        op1=ALU.add,
-                    )
-                nc.vector.tensor_scalar(
-                    out=lifted[:, POOL_FREQS * TERMS :], in0=angle[:, POOL_FREQS * TERMS :],
-                    scalar1=ROUND_MAGIC, scalar2=None, op0=ALU.add,
+            coef_t_of[u] = coef_t
+
+        def angles(u):
+            j = u // PAIRS
+            angle = work.tile(unit_shape, F32, name="angle")
+            for e in range(2):
+                jm = 2 * u + e
+                nc.scalar.activation(
+                    out=angle[:, e * TERMS : (e + 1) * TERMS],
+                    in_=xl_groups[:, j],
+                    func=ACT.Copy,
+                    scale=turns[:, jm : jm + 1],
                 )
-                minus_frac = work.tile([P, HALF_FREQS * TERMS, 2, 64], F32, name="minus_frac")
-                nc.vector.scalar_tensor_tensor(
-                    out=minus_frac[:].rearrange("p g b f -> p (g b f)"),
-                    in0=lifted[:].rearrange("p g b f -> p (g b f)"),
-                    scalar=ROUND_MAGIC,
-                    in1=angle[:].rearrange("p g b f -> p (g b f)"),
-                    op0=ALU.subtract,
-                    op1=ALU.subtract,
-                )
-                sine = work.tile([P, HALF_FREQS * TERMS, 2, 64], F32, name="sine")
-                nc.scalar.activation(out=sine[:], in_=minus_frac[:], func=ACT.Sin, scale=-2.0 * math.pi)
-                prod = work.tile([P, HALF_FREQS * TERMS, 2, 64], F32, name="prod")
-                nc.vector.tensor_tensor(
-                    out=prod[:],
-                    in0=sine[:],
-                    in1=coef_t[:].unsqueeze(2).to_broadcast([P, HALF_FREQS * TERMS, 2, 64]),
-                    op=ALU.mult,
-                )
-                for pair in range(2):
-                    for term in range(2 * TERMS):
-                        nc.tensor.matmul(
-                            out=summed[:, 2 * h + pair, :],
-                            lhsT=prod[:, pair * 2 * TERMS + term].rearrange("p b f -> p (b f)"),
-                            rhs=ident_f32[:],
-                            start=(term == 0),
-                            stop=(term == 2 * TERMS - 1),
-                            is_transpose=True,
-                        )
-            result = work.tile([P, 4, P], F32, name="result")
+            angle_of[u] = angle
+
+        def wholes(u):
+            whole = work.tile(unit_shape, F32, name="whole")
+            nc.vector.tensor_scalar(
+                out=whole[:], in0=angle_of[u][:], scalar1=ROUND_MAGIC, scalar2=ROUND_MAGIC,
+                op0=ALU.add, op1=ALU.subtract,
+            )
+            whole_of[u] = whole
+
+        def sines(u):
+            frac = work.tile(unit_shape, F32, name="frac")
             nc.vector.tensor_tensor(
-                out=result[:], in0=summed[:], in1=shift_sb[:, 4 * j : 4 * (j + 1), :], op=ALU.add
+                out=frac[:], in0=angle_of.pop(u)[:], in1=whole_of.pop(u)[:], op=ALU.subtract
+            )
+            sine = work.tile(unit_shape, F32, name="sine")
+            nc.scalar.activation(out=sine[:], in_=frac[:], func=ACT.Sin, scale=2.0 * math.pi)
+            sine_of[u] = sine
+
+        def products(u):
+            j, m2 = divmod(u, PAIRS)
+            if m2 == 0:
+                summed_of[j] = psum_sum.tile([P, PAIRS, P], F32, name="summed")
+            prod = work.tile(unit_shape, F32, name="prod")
+            nc.vector.tensor_tensor(
+                out=prod[:],
+                in0=sine_of.pop(u)[:],
+                in1=coef_t_of.pop(u)[:].unsqueeze(2).to_broadcast(unit_shape),
+                op=ALU.mult,
+            )
+            for term in range(2 * TERMS):
+                nc.tensor.matmul(
+                    out=summed_of[j][:, m2, :],
+                    lhsT=prod[:, term].rearrange("p b f -> p (b f)"),
+                    rhs=ident_f32[:],
+                    start=(term == 0),
+                    stop=(term == 2 * TERMS - 1),
+                    is_transpose=True,
+                )
+
+        def finish(j):
+            result = work.tile([P, PAIRS, P], F32, name="result")
+            nc.vector.tensor_tensor(
+                out=result[:], in0=summed_of.pop(j)[:], in1=shift_sb[:, PAIRS * j : PAIRS * (j + 1), :], op=ALU.add
             )
             for b in range(2):
                 nc.sync.dma_start(
-                    out=out_views[b][:, 4 * j : 4 * (j + 1), :], in_=result[64 * b : 64 * (b + 1)]
+                    out=out_views[b][:, PAIRS * j : PAIRS * (j + 1), :], in_=result[64 * b : 64 * (b + 1)]
                 )
+
+        for u in range(3):
+            angles(u)
+        for u in range(2):
+            coefficients(u)
+            wholes(u)
+        sines(0)
+        for u in range(UNITS):
+            if u + 3 < UNITS:
+                angles(u + 3)
+            if u + 2 < UNITS:
+                coefficients(u + 2)
+            if u + 1 < UNITS:
+                sines(u + 1)
+            if u + 2 < UNITS:
+                wholes(u + 2)
+            if u % PAIRS == 0 and u > 0:
+                finish(u // PAIRS - 1)
+            products(u)
+        finish(GROUPS - 1)

@@ -140,10 +140,11 @@ def tile_ka_attention_heads_mod_pa_s_kernel(
         out_views = [out[b].rearrange("h g p (d l) -> (p d) (h g) l", d=QUARTERS) for b in range(2)]
 
         angle_of = {}
-        whole_of = {}
+        lifted_of = {}
         coef_t_of = {}
         sine_of = {}
         summed_of = {}
+        shift_t_of = {}
 
         def coefficients(u):
             j, m2 = divmod(u, PAIRS)
@@ -170,22 +171,41 @@ def tile_ka_attention_heads_mod_pa_s_kernel(
                 )
             angle_of[u] = angle
 
-        def wholes(u):
-            whole = work.tile(unit_shape, F32, name="whole")
-            nc.vector.tensor_scalar(
-                out=whole[:], in0=angle_of[u][:], scalar1=ROUND_MAGIC, scalar2=ROUND_MAGIC,
-                op0=ALU.add, op1=ALU.subtract,
-            )
-            whole_of[u] = whole
+        def lifts(u):
+            j = u // PAIRS
+            lifted = work.tile(unit_shape, F32, name="lifted", bufs=2)
+            for e, engine in enumerate((nc.gpsimd, nc.vector)):
+                engine.tensor_scalar(
+                    out=lifted[:, e * TERMS : (e + 1) * TERMS],
+                    in0=xl_groups[:, j],
+                    scalar1=turns[:, 2 * u + e : 2 * u + e + 1],
+                    scalar2=ROUND_MAGIC,
+                    op0=ALU.mult,
+                    op1=ALU.add,
+                )
+            lifted_of[u] = lifted
 
         def sines(u):
-            frac = work.tile(unit_shape, F32, name="frac")
-            nc.vector.tensor_tensor(
-                out=frac[:], in0=angle_of.pop(u)[:], in1=whole_of.pop(u)[:], op=ALU.subtract
+            minus_frac = work.tile(unit_shape, F32, name="minus_frac")
+            nc.vector.scalar_tensor_tensor(
+                out=minus_frac[:].rearrange("p g b f -> p (g b f)"),
+                in0=lifted_of.pop(u)[:].rearrange("p g b f -> p (g b f)"),
+                scalar=ROUND_MAGIC,
+                in1=angle_of.pop(u)[:].rearrange("p g b f -> p (g b f)"),
+                op0=ALU.subtract,
+                op1=ALU.subtract,
             )
             sine = work.tile(unit_shape, F32, name="sine")
-            nc.scalar.activation(out=sine[:], in_=frac[:], func=ACT.Sin, scale=2.0 * math.pi)
+            nc.scalar.activation(out=sine[:], in_=minus_frac[:], func=ACT.Sin, scale=-2.0 * math.pi)
             sine_of[u] = sine
+
+        def shifts(j):
+            shift_ps = psum_setup.tile([P, PAIRS, P], BF16, name="shift_ps", tag="setup")
+            for m2 in range(PAIRS):
+                nc.tensor.transpose(shift_ps[:, m2, :], shift_sb[:, PAIRS * j + m2, :], ident_bf16[:])
+            shift_t = work.tile([P, PAIRS, P], F32, name="shift_t")
+            nc.scalar.copy(out=shift_t[:], in_=shift_ps[:])
+            shift_t_of[j] = shift_t
 
         def products(u):
             j, m2 = divmod(u, PAIRS)
@@ -198,21 +218,23 @@ def tile_ka_attention_heads_mod_pa_s_kernel(
                 in1=coef_t_of.pop(u)[:].unsqueeze(2).to_broadcast(unit_shape),
                 op=ALU.mult,
             )
+            nc.tensor.matmul(
+                out=summed_of[j][:, m2, :], lhsT=shift_t_of[j][:, m2, :], rhs=ident_f32[:],
+                start=True, stop=False, is_transpose=True,
+            )
             for term in range(2 * TERMS):
                 nc.tensor.matmul(
                     out=summed_of[j][:, m2, :],
                     lhsT=prod[:, term].rearrange("p b f -> p (b f)"),
                     rhs=ident_f32[:],
-                    start=(term == 0),
+                    start=False,
                     stop=(term == 2 * TERMS - 1),
                     is_transpose=True,
                 )
 
         def finish(j):
             result = work.tile([P, PAIRS, P], F32, name="result")
-            nc.vector.tensor_tensor(
-                out=result[:], in0=summed_of.pop(j)[:], in1=shift_sb[:, PAIRS * j : PAIRS * (j + 1), :], op=ALU.add
-            )
+            nc.scalar.copy(out=result[:], in_=summed_of.pop(j)[:])
             for b in range(2):
                 nc.sync.dma_start(
                     out=out_views[b][:, PAIRS * j : PAIRS * (j + 1), :], in_=result[64 * b : 64 * (b + 1)]
@@ -222,18 +244,23 @@ def tile_ka_attention_heads_mod_pa_s_kernel(
             angles(u)
         for u in range(2):
             coefficients(u)
-            wholes(u)
+            lifts(u)
+        shifts(0)
         sines(0)
+        lifts(2)
         for u in range(UNITS):
             if u + 3 < UNITS:
                 angles(u + 3)
             if u + 2 < UNITS:
                 coefficients(u + 2)
+            if u % PAIRS == 0:
+                if u > 0:
+                    finish(u // PAIRS - 1)
+                if u + PAIRS < UNITS:
+                    shifts(u // PAIRS + 1)
             if u + 1 < UNITS:
                 sines(u + 1)
-            if u + 2 < UNITS:
-                wholes(u + 2)
-            if u % PAIRS == 0 and u > 0:
-                finish(u // PAIRS - 1)
             products(u)
+            if u + 3 < UNITS:
+                lifts(u + 3)
         finish(GROUPS - 1)

@@ -144,7 +144,6 @@ def tile_ka_attention_heads_mod_pa_s_kernel(
         coef_t_of = {}
         sine_of = {}
         summed_of = {}
-        shift_t_of = {}
 
         def coefficients(u):
             j, m2 = divmod(u, PAIRS)
@@ -199,14 +198,6 @@ def tile_ka_attention_heads_mod_pa_s_kernel(
             nc.scalar.activation(out=sine[:], in_=minus_frac[:], func=ACT.Sin, scale=-2.0 * math.pi)
             sine_of[u] = sine
 
-        def shifts(j):
-            shift_ps = psum_setup.tile([P, PAIRS, P], BF16, name="shift_ps", tag="setup")
-            for m2 in range(PAIRS):
-                nc.tensor.transpose(shift_ps[:, m2, :], shift_sb[:, PAIRS * j + m2, :], ident_bf16[:])
-            shift_t = work.tile([P, PAIRS, P], F32, name="shift_t")
-            nc.scalar.copy(out=shift_t[:], in_=shift_ps[:])
-            shift_t_of[j] = shift_t
-
         def products(u):
             j, m2 = divmod(u, PAIRS)
             if m2 == 0:
@@ -218,23 +209,21 @@ def tile_ka_attention_heads_mod_pa_s_kernel(
                 in1=coef_t_of.pop(u)[:].unsqueeze(2).to_broadcast(unit_shape),
                 op=ALU.mult,
             )
-            nc.tensor.matmul(
-                out=summed_of[j][:, m2, :], lhsT=shift_t_of[j][:, m2, :], rhs=ident_f32[:],
-                start=True, stop=False, is_transpose=True,
-            )
             for term in range(2 * TERMS):
                 nc.tensor.matmul(
                     out=summed_of[j][:, m2, :],
                     lhsT=prod[:, term].rearrange("p b f -> p (b f)"),
                     rhs=ident_f32[:],
-                    start=False,
+                    start=(term == 0),
                     stop=(term == 2 * TERMS - 1),
                     is_transpose=True,
                 )
 
         def finish(j):
             result = work.tile([P, PAIRS, P], F32, name="result")
-            nc.scalar.copy(out=result[:], in_=summed_of.pop(j)[:])
+            nc.vector.tensor_tensor(
+                out=result[:], in0=summed_of.pop(j)[:], in1=shift_sb[:, PAIRS * j : PAIRS * (j + 1), :], op=ALU.add
+            )
             for b in range(2):
                 nc.sync.dma_start(
                     out=out_views[b][:, PAIRS * j : PAIRS * (j + 1), :], in_=result[64 * b : 64 * (b + 1)]
@@ -245,7 +234,6 @@ def tile_ka_attention_heads_mod_pa_s_kernel(
         for u in range(2):
             coefficients(u)
             lifts(u)
-        shifts(0)
         sines(0)
         lifts(2)
         for u in range(UNITS):
@@ -253,14 +241,11 @@ def tile_ka_attention_heads_mod_pa_s_kernel(
                 angles(u + 3)
             if u + 2 < UNITS:
                 coefficients(u + 2)
-            if u % PAIRS == 0:
-                if u > 0:
-                    finish(u // PAIRS - 1)
-                if u + PAIRS < UNITS:
-                    shifts(u // PAIRS + 1)
             if u + 1 < UNITS:
                 sines(u + 1)
             products(u)
+            if u % PAIRS == 0 and u > 0:
+                finish(u // PAIRS - 1)
             if u + 3 < UNITS:
                 lifts(u + 3)
         finish(GROUPS - 1)

@@ -25,7 +25,8 @@ QUARTERS = 4
 PAIRS = FREQS // 2
 UNITS = GROUPS * PAIRS
 TERMS = 4
-ROUND_MAGIC = 12582912.0
+FRAC_LEAD = 3
+ROUND_LEAD = 5
 
 FLOPS = 2 * ROWS * K * COLS
 
@@ -34,7 +35,8 @@ def tile_ka_attention_heads_mod_pa_s_kernel(
     tc, x, lin_w_words, lin_w_scales, lin_b, grid, coef, shift, out
 ):
     nc = tc.nc
-    unit_shape = [P, 2 * TERMS, 2, 64]
+    unit_shape = [P, 2 * TERMS, P]
+    half = TERMS * P
     with ExitStack() as stack:
         keep = stack.enter_context(tc.tile_pool(name="keep", bufs=1))
         work = stack.enter_context(tc.tile_pool(name="work", bufs=3))
@@ -74,7 +76,7 @@ def tile_ka_attention_heads_mod_pa_s_kernel(
         shift_sb = keep.tile([P, PAIRS * GROUPS, P], BF16, name="shift_sb")
         shift_view = shift[0].rearrange("h g p (d l) -> (p d) (h g) l", d=QUARTERS)
         for b in range(2):
-            nc.sync.dma_start(out=shift_sb[64 * b : 64 * (b + 1)], in_=shift_view)
+            nc.sync.dma_start(out=shift_sb[b:P:2], in_=shift_view)
 
         ident_f32 = keep.tile([P, P], F32, name="ident_f32")
         make_identity(nc, ident_f32[:])
@@ -92,8 +94,8 @@ def tile_ka_attention_heads_mod_pa_s_kernel(
             nc.tensor.transpose(x_t[:, u, :], x_words[:, u : K // 2 : 2], ident_f32[:])
         grouped = keep.tile([P, ROWS, 4], BF16, name="grouped", align_bytes=64)
         nc.vector.tensor_copy(
-            out=grouped[:].rearrange("p r t -> p (r t)").bitcast(F32).rearrange("p (r u) -> p r u", u=2),
-            in_=x_t[:].rearrange("p u r -> p r u"),
+            out=grouped[:].rearrange("p q t -> p (q t)").bitcast(F32).rearrange("p (r b u) -> p r b u", b=2, u=2),
+            in_=x_t[:].rearrange("p u (b r) -> p r b u", b=2),
         )
         x_codes = keep.tile([P, ROWS], U32, name="x_codes", align_bytes=64)
         x_scales = keep.tile([P, ROWS], U8, name="x_scales", align_bytes=64)
@@ -113,7 +115,7 @@ def tile_ka_attention_heads_mod_pa_s_kernel(
             op0=ALU.mult, op1=ALU.add,
         )
 
-        xl = keep.tile([P, ROWS, CHUNKS, QUARTERS], F32, name="xl")
+        xl = keep.tile([P, ROWS // 2, CHUNKS, QUARTERS, 2], F32, name="xl")
         for cc in range(CHUNKS):
             acc = psum_setup.tile([P, QUARTERS, ROWS], F32, name="acc", tag="setup")
             for dq in range(QUARTERS):
@@ -128,19 +130,17 @@ def tile_ka_attention_heads_mod_pa_s_kernel(
                     stop=True,
                 )
             nc.vector.tensor_tensor(
-                out=xl[:, :, cc, :],
-                in0=acc[:].rearrange("p d n -> p n d"),
-                in1=bias_t[:, cc * QUARTERS : (cc + 1) * QUARTERS].unsqueeze(1).to_broadcast([P, ROWS, QUARTERS]),
+                out=xl[:, :, cc, :, :],
+                in0=acc[:].rearrange("p d (r b) -> p r d b", b=2),
+                in1=bias_t[:, cc * QUARTERS : (cc + 1) * QUARTERS].unsqueeze(1).unsqueeze(3).to_broadcast([P, ROWS // 2, QUARTERS, 2]),
                 op=ALU.add,
             )
-        xl_groups = xl[:].rearrange("p n c d -> p (n c d)").rearrange(
-            "p (b j a f) -> p j a b f", b=2, j=GROUPS, a=TERMS
-        )
+        xl_groups = xl[:].rearrange("p r c d b -> p (r c d b)").rearrange("p (j f) -> p j f", j=GROUPS)
         coef_cols = coef_sb[:].rearrange("p a (l m j) -> p a l m j", m=FREQS, j=GROUPS)
         out_views = [out[b].rearrange("h g p (d l) -> (p d) (h g) l", d=QUARTERS) for b in range(2)]
 
-        angle_of = {}
-        lifted_of = {}
+        whole_of = {}
+        frac_of = {}
         coef_t_of = {}
         sine_of = {}
         summed_of = {}
@@ -157,45 +157,38 @@ def tile_ka_attention_heads_mod_pa_s_kernel(
                     )
             coef_t_of[u] = coef_t
 
-        def angles(u):
+        def rounds(u, engine):
             j = u // PAIRS
-            angle = work.tile(unit_shape, F32, name="angle")
+            whole = work.tile([P, 2 * half], I32, name="whole", bufs=4)
             for e in range(2):
-                jm = 2 * u + e
-                nc.scalar.activation(
-                    out=angle[:, e * TERMS : (e + 1) * TERMS],
-                    in_=xl_groups[:, j],
-                    func=ACT.Copy,
-                    scale=turns[:, jm : jm + 1],
-                )
-            angle_of[u] = angle
-
-        def lifts(u):
-            j = u // PAIRS
-            lifted = work.tile(unit_shape, F32, name="lifted", bufs=2)
-            for e, engine in enumerate((nc.gpsimd, nc.vector)):
                 engine.tensor_scalar(
-                    out=lifted[:, e * TERMS : (e + 1) * TERMS],
+                    out=whole[:, e * half : (e + 1) * half],
                     in0=xl_groups[:, j],
                     scalar1=turns[:, 2 * u + e : 2 * u + e + 1],
-                    scalar2=ROUND_MAGIC,
+                    scalar2=0.0,
                     op0=ALU.mult,
                     op1=ALU.add,
                 )
-            lifted_of[u] = lifted
+            whole_of[u] = whole
+
+        def fracs(u):
+            j = u // PAIRS
+            whole = whole_of.pop(u)
+            frac = work.tile([P, 2 * half], F32, name="frac")
+            for e in range(2):
+                nc.vector.scalar_tensor_tensor(
+                    out=frac[:, e * half : (e + 1) * half],
+                    in0=xl_groups[:, j],
+                    scalar=turns[:, 2 * u + e : 2 * u + e + 1],
+                    in1=whole[:, e * half : (e + 1) * half],
+                    op0=ALU.mult,
+                    op1=ALU.subtract,
+                )
+            frac_of[u] = frac
 
         def sines(u):
-            minus_frac = work.tile(unit_shape, F32, name="minus_frac")
-            nc.vector.scalar_tensor_tensor(
-                out=minus_frac[:].rearrange("p g b f -> p (g b f)"),
-                in0=lifted_of.pop(u)[:].rearrange("p g b f -> p (g b f)"),
-                scalar=ROUND_MAGIC,
-                in1=angle_of.pop(u)[:].rearrange("p g b f -> p (g b f)"),
-                op0=ALU.subtract,
-                op1=ALU.subtract,
-            )
-            sine = work.tile(unit_shape, F32, name="sine")
-            nc.scalar.activation(out=sine[:], in_=minus_frac[:], func=ACT.Sin, scale=-2.0 * math.pi)
+            sine = work.tile([P, 2 * half], F32, name="sine", bufs=5)
+            nc.scalar.activation(out=sine[:], in_=frac_of.pop(u)[:], func=ACT.Sin, scale=2.0 * math.pi)
             sine_of[u] = sine
 
         def products(u):
@@ -204,15 +197,15 @@ def tile_ka_attention_heads_mod_pa_s_kernel(
                 summed_of[j] = psum_sum.tile([P, PAIRS, P], F32, name="summed")
             prod = work.tile(unit_shape, F32, name="prod")
             nc.vector.tensor_tensor(
-                out=prod[:],
-                in0=sine_of.pop(u)[:],
-                in1=coef_t_of.pop(u)[:].unsqueeze(2).to_broadcast(unit_shape),
+                out=prod[:].rearrange("p g (f b) -> p (g f) b", b=2),
+                in0=sine_of.pop(u)[:].rearrange("p (f b) -> p f b", b=2),
+                in1=coef_t_of.pop(u)[:].rearrange("p g f -> p (g f)").unsqueeze(2).to_broadcast([P, half, 2]),
                 op=ALU.mult,
             )
             for term in range(2 * TERMS):
                 nc.tensor.matmul(
                     out=summed_of[j][:, m2, :],
-                    lhsT=prod[:, term].rearrange("p b f -> p (b f)"),
+                    lhsT=prod[:, term, :],
                     rhs=ident_f32[:],
                     start=(term == 0),
                     stop=(term == 2 * TERMS - 1),
@@ -225,27 +218,21 @@ def tile_ka_attention_heads_mod_pa_s_kernel(
                 out=result[:], in0=summed_of.pop(j)[:], in1=shift_sb[:, PAIRS * j : PAIRS * (j + 1), :], op=ALU.add
             )
             for b in range(2):
-                nc.sync.dma_start(
-                    out=out_views[b][:, PAIRS * j : PAIRS * (j + 1), :], in_=result[64 * b : 64 * (b + 1)]
-                )
+                nc.sync.dma_start(out=out_views[b][:, PAIRS * j : PAIRS * (j + 1), :], in_=result[b:P:2])
 
-        for u in range(3):
-            angles(u)
-        for u in range(2):
-            coefficients(u)
-            lifts(u)
-        sines(0)
-        lifts(2)
-        for u in range(UNITS):
-            if u + 3 < UNITS:
-                angles(u + 3)
-            if u + 2 < UNITS:
-                coefficients(u + 2)
-            if u + 1 < UNITS:
-                sines(u + 1)
-            products(u)
-            if u % PAIRS == 0 and u > 0:
-                finish(u // PAIRS - 1)
-            if u + 3 < UNITS:
-                lifts(u + 3)
+        rounds(0, nc.vector)
+        for u in range(1, ROUND_LEAD - FRAC_LEAD):
+            rounds(u, nc.gpsimd)
+        for step in range(-FRAC_LEAD, UNITS):
+            if step + ROUND_LEAD < UNITS:
+                rounds(step + ROUND_LEAD, nc.gpsimd)
+            if 0 <= step + 2 < UNITS:
+                coefficients(step + 2)
+            if step + FRAC_LEAD < UNITS:
+                fracs(step + FRAC_LEAD)
+                sines(step + FRAC_LEAD)
+            if step >= 0:
+                products(step)
+                if step % PAIRS == 0 and step > 0:
+                    finish(step // PAIRS - 1)
         finish(GROUPS - 1)

@@ -140,6 +140,8 @@ def tile_ka_attention_heads_mod_pa_s_kernel(
         out_views = [out[b].rearrange("h g p (d l) -> (p d) (h g) l", d=QUARTERS) for b in range(2)]
 
         whole_of = {}
+        flipped_of = {}
+        group_of = {}
         frac_of = {}
         coef_t_of = {}
         sine_of = {}
@@ -156,6 +158,21 @@ def tile_ka_attention_heads_mod_pa_s_kernel(
                         ident_bf16[:],
                     )
             coef_t_of[u] = coef_t
+
+        def flip(j):
+            flipped_ps = psum_setup.tile([P, TERMS, P], F32, name="flipped_ps", tag="setup")
+            for a in range(TERMS):
+                nc.tensor.transpose(flipped_ps[:, a, :], xl_groups[:, j, a * P : (a + 1) * P], ident_f32[:])
+            flipped = work.tile([P, TERMS, P], F32, name="flipped", bufs=2)
+            nc.scalar.copy(out=flipped[:], in_=flipped_ps[:])
+            flipped_of[j] = flipped
+
+        def flip_back(j):
+            flipped = flipped_of.pop(j)
+            group = psum_setup.tile([P, TERMS, P], F32, name="group", tag="setup")
+            for a in range(TERMS):
+                nc.tensor.transpose(group[:, a, :], flipped[:, a, :], ident_f32[:])
+            group_of[j] = group
 
         def rounds(u, engine):
             j = u // PAIRS
@@ -178,7 +195,7 @@ def tile_ka_attention_heads_mod_pa_s_kernel(
             for e in range(2):
                 nc.vector.scalar_tensor_tensor(
                     out=frac[:, e * half : (e + 1) * half],
-                    in0=xl_groups[:, j],
+                    in0=group_of[j][:].rearrange("p a f -> p (a f)"),
                     scalar=turns[:, 2 * u + e : 2 * u + e + 1],
                     in1=whole[:, e * half : (e + 1) * half],
                     op0=ALU.mult,
@@ -220,12 +237,17 @@ def tile_ka_attention_heads_mod_pa_s_kernel(
             for b in range(2):
                 nc.sync.dma_start(out=out_views[b][:, PAIRS * j : PAIRS * (j + 1), :], in_=result[b:P:2])
 
-        rounds(0, nc.vector)
-        for u in range(1, ROUND_LEAD - FRAC_LEAD):
+        flip(0)
+        flip_back(0)
+        for u in range(ROUND_LEAD - FRAC_LEAD):
             rounds(u, nc.gpsimd)
         for step in range(-FRAC_LEAD, UNITS):
             if step + ROUND_LEAD < UNITS:
                 rounds(step + ROUND_LEAD, nc.gpsimd)
+            if (step + 6) % PAIRS == 0 and 0 < (step + 6) // PAIRS < GROUPS:
+                flip((step + 6) // PAIRS)
+            if (step + 5) % PAIRS == 0 and 0 < (step + 5) // PAIRS < GROUPS:
+                flip_back((step + 5) // PAIRS)
             if 0 <= step + 2 < UNITS:
                 coefficients(step + 2)
             if step + FRAC_LEAD < UNITS:

@@ -27,6 +27,7 @@ UNITS = GROUPS * PAIRS
 TERMS = 4
 FRAC_LEAD = 3
 ROUND_LEAD = 5
+GPSIMD_EVERY = 4
 
 FLOPS = 2 * ROWS * K * COLS
 
@@ -146,6 +147,8 @@ def tile_ka_attention_heads_mod_pa_s_kernel(
         coef_t_of = {}
         sine_of = {}
         summed_of = {}
+        spread_of = {}
+        prod_of = {}
 
         def coefficients(u):
             j, m2 = divmod(u, PAIRS)
@@ -208,17 +211,41 @@ def tile_ka_attention_heads_mod_pa_s_kernel(
             nc.scalar.activation(out=sine[:], in_=frac_of.pop(u)[:], func=ACT.Sin, scale=2.0 * math.pi)
             sine_of[u] = sine
 
+        def on_gpsimd(u):
+            return u % GPSIMD_EVERY == GPSIMD_EVERY - 1
+
+        def spread(u):
+            twice = work.tile([P, half, 2], BF16, name="twice", bufs=2)
+            nc.scalar.copy(
+                out=twice[:],
+                in_=coef_t_of.pop(u)[:].rearrange("p g f -> p (g f)").unsqueeze(2).to_broadcast([P, half, 2]),
+            )
+            spread_of[u] = twice
+
+        def products_gpsimd(u):
+            prod = work.tile(unit_shape, F32, name="prod_g", bufs=2)
+            nc.gpsimd.tensor_tensor(
+                out=prod[:].rearrange("p g f -> p (g f)"),
+                in0=sine_of.pop(u)[:],
+                in1=spread_of.pop(u)[:].rearrange("p f b -> p (f b)"),
+                op=ALU.mult,
+            )
+            prod_of[u] = prod
+
         def products(u):
             j, m2 = divmod(u, PAIRS)
             if m2 == 0:
                 summed_of[j] = psum_sum.tile([P, PAIRS, P], F32, name="summed")
-            prod = work.tile(unit_shape, F32, name="prod")
-            nc.vector.tensor_tensor(
-                out=prod[:].rearrange("p g (f b) -> p (g f) b", b=2),
-                in0=sine_of.pop(u)[:].rearrange("p (f b) -> p f b", b=2),
-                in1=coef_t_of.pop(u)[:].rearrange("p g f -> p (g f)").unsqueeze(2).to_broadcast([P, half, 2]),
-                op=ALU.mult,
-            )
+            if on_gpsimd(u):
+                prod = prod_of.pop(u)
+            else:
+                prod = work.tile(unit_shape, F32, name="prod")
+                nc.vector.tensor_tensor(
+                    out=prod[:].rearrange("p g (f b) -> p (g f) b", b=2),
+                    in0=sine_of.pop(u)[:].rearrange("p (f b) -> p f b", b=2),
+                    in1=coef_t_of.pop(u)[:].rearrange("p g f -> p (g f)").unsqueeze(2).to_broadcast([P, half, 2]),
+                    op=ALU.mult,
+                )
             for term in range(2 * TERMS):
                 nc.tensor.matmul(
                     out=summed_of[j][:, m2, :],
@@ -248,8 +275,9 @@ def tile_ka_attention_heads_mod_pa_s_kernel(
                 flip((step + 6) // PAIRS)
             if (step + 5) % PAIRS == 0 and 0 < (step + 5) // PAIRS < GROUPS:
                 flip_back((step + 5) // PAIRS)
-            if 0 <= step + 2 < UNITS:
-                coefficients(step + 2)
+            if 0 <= step + 2 < UNITS and on_gpsimd(step + 2):
+                spread(step + 2)
+                products_gpsimd(step + 2)
             if step + FRAC_LEAD < UNITS:
                 fracs(step + FRAC_LEAD)
                 sines(step + FRAC_LEAD)
@@ -257,4 +285,6 @@ def tile_ka_attention_heads_mod_pa_s_kernel(
                 products(step)
                 if step % PAIRS == 0 and step > 0:
                     finish(step // PAIRS - 1)
+            if step + 3 < UNITS:
+                coefficients(step + 3)
         finish(GROUPS - 1)

@@ -25,9 +25,9 @@ QUARTERS = 4
 PAIRS = FREQS // 2
 UNITS = GROUPS * PAIRS
 TERMS = 4
-FRAC_LEAD = 3
-ROUND_LEAD = 5
-GPSIMD_EVERY = 4
+ROUND_AHEAD = 2
+GPSIMD_UNITS = (14, 17)
+SPREAD_AFTER = {4: 14, 6: 17}
 
 FLOPS = 2 * ROWS * K * COLS
 
@@ -74,10 +74,10 @@ def tile_ka_attention_heads_mod_pa_s_kernel(
         for a in range(2):
             nc.sync.dma_start(out=coef_sb[:, a, :], in_=coef_halves[a])
 
-        shift_sb = keep.tile([P, PAIRS * GROUPS, P], BF16, name="shift_sb")
-        shift_view = shift[0].rearrange("h g p (d l) -> (p d) (h g) l", d=QUARTERS)
-        for b in range(2):
-            nc.sync.dma_start(out=shift_sb[b:P:2], in_=shift_view)
+        shift_sb = keep.tile([P, UNITS // 2, P], BF16, name="shift_sb")
+        shift_view = shift[0].rearrange("h g p (d l) -> (h g) (p d) l", d=QUARTERS).rearrange("(w s) q l -> s q w l", s=2)
+        for s in range(2):
+            nc.sync.dma_start(out=shift_sb[64 * s : 64 * (s + 1)], in_=shift_view[s])
 
         ident_f32 = keep.tile([P, P], F32, name="ident_f32")
         make_identity(nc, ident_f32[:])
@@ -162,6 +162,22 @@ def tile_ka_attention_heads_mod_pa_s_kernel(
                     )
             coef_t_of[u] = coef_t
 
+        shift_t = keep.tile([P, UNITS, P], F32, name="shift_t")
+        shift_ps_of = {}
+
+        def shift_flip(k):
+            shift_ps = psum_sum.tile([P, UNITS // 4, P], BF16, name="shift_ps", tag="summed")
+            for w in range(UNITS // 4):
+                nc.tensor.transpose(shift_ps[:, w, :], shift_sb[:, k * (UNITS // 4) + w, :], ident_bf16[:])
+            shift_ps_of[k] = shift_ps
+
+        def shift_spread(k):
+            count = UNITS // 2 * 64
+            nc.scalar.copy(
+                out=shift_t[:, k * (UNITS // 2) : (k + 1) * (UNITS // 2), :].rearrange("p u (q b) -> p (u q) b", b=2),
+                in_=shift_ps_of.pop(k)[:].rearrange("p w q -> p (w q)").unsqueeze(2).to_broadcast([P, count, 2]),
+            )
+
         def flip(j):
             flipped_ps = psum_setup.tile([P, TERMS, P], F32, name="flipped_ps", tag="setup")
             for a in range(TERMS):
@@ -207,12 +223,12 @@ def tile_ka_attention_heads_mod_pa_s_kernel(
             frac_of[u] = frac
 
         def sines(u):
-            sine = work.tile([P, 2 * half], F32, name="sine", bufs=5)
+            sine = work.tile([P, 2 * half], F32, name="sine", bufs=10)
             nc.scalar.activation(out=sine[:], in_=frac_of.pop(u)[:], func=ACT.Sin, scale=2.0 * math.pi)
             sine_of[u] = sine
 
         def on_gpsimd(u):
-            return u % GPSIMD_EVERY == GPSIMD_EVERY - 1
+            return u in GPSIMD_UNITS
 
         def spread(u):
             twice = work.tile([P, half, 2], BF16, name="twice", bufs=2)
@@ -235,7 +251,7 @@ def tile_ka_attention_heads_mod_pa_s_kernel(
         def products(u):
             j, m2 = divmod(u, PAIRS)
             if m2 == 0:
-                summed_of[j] = psum_sum.tile([P, PAIRS, P], F32, name="summed")
+                summed_of[j] = psum_sum.tile([P, PAIRS, P], F32, name="summed", tag="summed")
             if on_gpsimd(u):
                 prod = prod_of.pop(u)
             else:
@@ -246,45 +262,59 @@ def tile_ka_attention_heads_mod_pa_s_kernel(
                     in1=coef_t_of.pop(u)[:].rearrange("p g f -> p (g f)").unsqueeze(2).to_broadcast([P, half, 2]),
                     op=ALU.mult,
                 )
-            for term in range(2 * TERMS):
+            for term in range(2 * TERMS + 1):
                 nc.tensor.matmul(
                     out=summed_of[j][:, m2, :],
-                    lhsT=prod[:, term, :],
+                    lhsT=prod[:, term, :] if term < 2 * TERMS else shift_t[:, u, :],
                     rhs=ident_f32[:],
                     start=(term == 0),
-                    stop=(term == 2 * TERMS - 1),
+                    stop=(term == 2 * TERMS),
                     is_transpose=True,
                 )
 
         def finish(j):
             result = work.tile([P, PAIRS, P], F32, name="result")
-            nc.vector.tensor_tensor(
-                out=result[:], in0=summed_of.pop(j)[:], in1=shift_sb[:, PAIRS * j : PAIRS * (j + 1), :], op=ALU.add
-            )
+            nc.scalar.copy(out=result[:], in_=summed_of.pop(j)[:])
             for b in range(2):
                 nc.sync.dma_start(out=out_views[b][:, PAIRS * j : PAIRS * (j + 1), :], in_=result[b:P:2])
 
+        def product_stage(u):
+            products(u)
+            if u % PAIRS == 0 and u > 0:
+                finish(u // PAIRS - 1)
+            if u in SPREAD_AFTER:
+                coefficients(SPREAD_AFTER[u])
+                spread(SPREAD_AFTER[u])
+            later = [v for v in range(u + 1, UNITS) if not on_gpsimd(v)]
+            if not on_gpsimd(u) and len(later) >= 3:
+                coefficients(later[2])
+
         flip(0)
         flip_back(0)
-        for u in range(ROUND_LEAD - FRAC_LEAD):
+        for u in range(ROUND_AHEAD):
             rounds(u, nc.gpsimd)
-        for step in range(-FRAC_LEAD, UNITS):
-            if step + ROUND_LEAD < UNITS:
-                rounds(step + ROUND_LEAD, nc.gpsimd)
-            if (step + 6) % PAIRS == 0 and 0 < (step + 6) // PAIRS < GROUPS:
-                flip((step + 6) // PAIRS)
-            if (step + 5) % PAIRS == 0 and 0 < (step + 5) // PAIRS < GROUPS:
-                flip_back((step + 5) // PAIRS)
-            if 0 <= step + 2 < UNITS and on_gpsimd(step + 2):
-                spread(step + 2)
-                products_gpsimd(step + 2)
-            if step + FRAC_LEAD < UNITS:
-                fracs(step + FRAC_LEAD)
-                sines(step + FRAC_LEAD)
-            if step >= 0:
-                products(step)
-                if step % PAIRS == 0 and step > 0:
-                    finish(step // PAIRS - 1)
-            if step + 3 < UNITS:
-                coefficients(step + 3)
+        made = 0
+        for w in range(UNITS):
+            if w + ROUND_AHEAD < UNITS:
+                rounds(w + ROUND_AHEAD, nc.gpsimd)
+            fracs(w)
+            sines(w)
+            if (w + 4) % PAIRS == 0 and (w + 4) // PAIRS < GROUPS:
+                flip((w + 4) // PAIRS)
+            if (w + 3) % PAIRS == 0 and (w + 3) // PAIRS < GROUPS:
+                flip_back((w + 3) // PAIRS)
+            if w == 0:
+                for u in range(3):
+                    coefficients(u)
+                for k in range(2):
+                    shift_flip(k)
+            if w in (1, 2):
+                shift_spread(w - 1)
+            for u in range(made, 2 * w // 3):
+                product_stage(u)
+            made = max(made, 2 * w // 3)
+        for u in GPSIMD_UNITS:
+            products_gpsimd(u)
+        for u in range(made, UNITS):
+            product_stage(u)
         finish(GROUPS - 1)

@@ -49,6 +49,8 @@ def tile_ka_attention_heads_mod_pa_s_kernel(
         x_sb = keep.tile([P, K], BF16, name="x_sb")
         nc.sync.dma_start(out=x_sb[:], in_=x.flatten_outer_dims())
 
+        w_words = keep.tile([P, 2 * COLS], U8, name="w_words", align_bytes=64)
+        nc.sync.dma_start(out=w_words[:].bitcast(I32), in_=lin_w_words[0].bitcast(I32))
         w_planes = keep.tile([P, COLS], U8, name="w_planes", align_bytes=64)
         nc.vector.memset(w_planes[:].bitcast(I32), 0)
         scale_rows = lin_w_scales[0].rearrange("(q r) n -> r q n", r=4)
@@ -56,18 +58,17 @@ def tile_ka_attention_heads_mod_pa_s_kernel(
             nc.sync.dma_start(
                 out=w_planes[r:P:32, :].bitcast(I32), in_=scale_rows[r].bitcast(I32)
             )
-        w_words = keep.tile([P, 2 * COLS], U8, name="w_words", align_bytes=64)
-        nc.sync.dma_start(out=w_words[:].bitcast(I32), in_=lin_w_words[0].bitcast(I32))
 
         bias_rows = keep.tile([P, P], BF16, name="bias_rows")
         nc.vector.memset(bias_rows[:], 0.0)
-        nc.scalar.dma_start(
-            out=bias_rows[0 : COLS // P, :], in_=lin_b.rearrange("(r c) -> r c", c=P)
-        )
-        grid_all = keep.tile([P, GROUPS * FREQS], BF16, name="grid_all")
-        nc.scalar.dma_start(
-            out=grid_all[:], in_=grid.rearrange("g f -> (g f)").partition_broadcast(P)
-        )
+        bias_view = lin_b.rearrange("(r c) -> r c", c=P)
+        nc.scalar.dma_start(out=bias_rows[0:16, :], in_=bias_view[0:16, :])
+        nc.scalar.dma_start(out=bias_rows[16 : COLS // P, :], in_=bias_view[16 : COLS // P, :])
+        grid_rows = keep.tile([P, GROUPS * FREQS], BF16, name="grid_rows")
+        nc.vector.memset(grid_rows[:], 0.0)
+        nc.scalar.dma_start(out=grid_rows[0:1, :], in_=grid.rearrange("(o g) f -> o (g f)", o=1))
+        ones = keep.tile([P, P], BF16, name="ones")
+        nc.vector.memset(ones[:], 1.0)
 
         coef_sb = keep.tile([P, 2, P * FREQS * GROUPS], BF16, name="coef_sb")
         coef_halves = coef.rearrange("(a p l) m j -> a p (l m j)", a=2, p=P)
@@ -110,11 +111,10 @@ def tile_ka_attention_heads_mod_pa_s_kernel(
         nc.tensor.transpose(bias_ps[:], bias_rows[:], ident_bf16[:])
         bias_t = keep.tile([P, COLS // P], F32, name="bias_t")
         nc.vector.tensor_copy(out=bias_t[:], in_=bias_ps[:, 0 : COLS // P])
+        grid_ps = psum_setup.tile([P, GROUPS * FREQS], F32, name="grid_ps", tag="setup")
+        nc.tensor.matmul(out=grid_ps[:], lhsT=ones[:], rhs=grid_rows[:], start=True, stop=True)
         turns = keep.tile([P, GROUPS * FREQS], F32, name="turns")
-        nc.gpsimd.tensor_scalar(
-            out=turns[:], in0=grid_all[:], scalar1=1.0 / (2.0 * math.pi), scalar2=0.0,
-            op0=ALU.mult, op1=ALU.add,
-        )
+        nc.scalar.activation(out=turns[:], in_=grid_ps[:], func=ACT.Copy, scale=1.0 / (2.0 * math.pi))
 
         xl = keep.tile([P, ROWS // 2, CHUNKS, QUARTERS, 2], F32, name="xl")
         for cc in range(CHUNKS):

@@ -75,10 +75,10 @@ def tile_ka_attention_heads_mod_pa_s_kernel(
         for a in range(2):
             nc.sync.dma_start(out=coef_sb[:, a, :], in_=coef_halves[a])
 
-        shift_sb = keep.tile([P, UNITS // 2, P], BF16, name="shift_sb")
-        shift_view = shift[0].rearrange("h g p (d l) -> (h g) (p d) l", d=QUARTERS).rearrange("(w s) q l -> s q w l", s=2)
-        for s in range(2):
-            nc.sync.dma_start(out=shift_sb[64 * s : 64 * (s + 1)], in_=shift_view[s])
+        shift_sb = keep.tile([P, UNITS, P], BF16, name="shift_sb")
+        shift_view = shift[0].rearrange("h g p (d l) -> (p d) (h g) l", d=QUARTERS)
+        for b in range(2):
+            nc.sync.dma_start(out=shift_sb[b:P:2], in_=shift_view)
 
         ident_f32 = keep.tile([P, P], F32, name="ident_f32")
         make_identity(nc, ident_f32[:])
@@ -149,6 +149,7 @@ def tile_ka_attention_heads_mod_pa_s_kernel(
         summed_of = {}
         spread_of = {}
         prod_of = {}
+        sums_of = {}
 
         def coefficients(u):
             j, m2 = divmod(u, PAIRS)
@@ -161,22 +162,6 @@ def tile_ka_attention_heads_mod_pa_s_kernel(
                         ident_bf16[:],
                     )
             coef_t_of[u] = coef_t
-
-        shift_t = keep.tile([P, UNITS, P], F32, name="shift_t")
-        shift_ps_of = {}
-
-        def shift_flip(k):
-            shift_ps = psum_sum.tile([P, UNITS // 4, P], BF16, name="shift_ps", tag="summed")
-            for w in range(UNITS // 4):
-                nc.tensor.transpose(shift_ps[:, w, :], shift_sb[:, k * (UNITS // 4) + w, :], ident_bf16[:])
-            shift_ps_of[k] = shift_ps
-
-        def shift_spread(k):
-            count = UNITS // 2 * 64
-            nc.scalar.copy(
-                out=shift_t[:, k * (UNITS // 2) : (k + 1) * (UNITS // 2), :].rearrange("p u (q b) -> p (u q) b", b=2),
-                in_=shift_ps_of.pop(k)[:].rearrange("p w q -> p (w q)").unsqueeze(2).to_broadcast([P, count, 2]),
-            )
 
         def flip(j):
             flipped_ps = psum_setup.tile([P, TERMS, P], F32, name="flipped_ps", tag="setup")
@@ -262,19 +247,30 @@ def tile_ka_attention_heads_mod_pa_s_kernel(
                     in1=coef_t_of.pop(u)[:].rearrange("p g f -> p (g f)").unsqueeze(2).to_broadcast([P, half, 2]),
                     op=ALU.mult,
                 )
-            for term in range(2 * TERMS + 1):
+            for term in range(2 * TERMS):
                 nc.tensor.matmul(
                     out=summed_of[j][:, m2, :],
-                    lhsT=prod[:, term, :] if term < 2 * TERMS else shift_t[:, u, :],
+                    lhsT=prod[:, term, :],
                     rhs=ident_f32[:],
                     start=(term == 0),
-                    stop=(term == 2 * TERMS),
+                    stop=(term == 2 * TERMS - 1),
                     is_transpose=True,
                 )
 
         def finish(j):
+            sums = work.tile([P, PAIRS * P], F32, name="sums", bufs=GROUPS - 1)
+            nc.scalar.copy(out=sums[:], in_=summed_of.pop(j)[:].rearrange("p g f -> p (g f)"))
+            sums_of[j] = sums
+
+        def shifted(j, engine):
+            sums = sums_of.pop(j)[:] if j in sums_of else summed_of.pop(j)[:].rearrange("p g f -> p (g f)")
             result = work.tile([P, PAIRS, P], F32, name="result")
-            nc.scalar.copy(out=result[:], in_=summed_of.pop(j)[:])
+            engine.tensor_tensor(
+                out=result[:].rearrange("p g f -> p (g f)"),
+                in0=sums,
+                in1=shift_sb[:, PAIRS * j : PAIRS * (j + 1), :].rearrange("p g f -> p (g f)"),
+                op=ALU.add,
+            )
             for b in range(2):
                 nc.sync.dma_start(out=out_views[b][:, PAIRS * j : PAIRS * (j + 1), :], in_=result[b:P:2])
 
@@ -306,10 +302,6 @@ def tile_ka_attention_heads_mod_pa_s_kernel(
             if w == 0:
                 for u in range(3):
                     coefficients(u)
-                for k in range(2):
-                    shift_flip(k)
-            if w in (1, 2):
-                shift_spread(w - 1)
             for u in range(made, 2 * w // 3):
                 product_stage(u)
             made = max(made, 2 * w // 3)
@@ -317,4 +309,7 @@ def tile_ka_attention_heads_mod_pa_s_kernel(
             products_gpsimd(u)
         for u in range(made, UNITS):
             product_stage(u)
-        finish(GROUPS - 1)
+            if u == UNITS - 2:
+                for j in range(GROUPS - 1):
+                    shifted(j, nc.gpsimd)
+        shifted(GROUPS - 1, nc.vector)

@@ -27,6 +27,7 @@ UNITS = GROUPS * PAIRS
 TERMS = 4
 ROUND_AHEAD = 2
 GPSIMD_UNITS = (14, 17)
+ADD_LAG = 3
 SPREAD_AFTER = {4: 14, 6: 17}
 
 FLOPS = 2 * ROWS * K * COLS
@@ -216,19 +217,16 @@ def tile_ka_attention_heads_mod_pa_s_kernel(
             return u in GPSIMD_UNITS
 
         def spread(u):
-            twice = work.tile([P, half, 2], BF16, name="twice", bufs=2)
-            nc.scalar.copy(
-                out=twice[:],
-                in_=coef_t_of.pop(u)[:].rearrange("p g f -> p (g f)").unsqueeze(2).to_broadcast([P, half, 2]),
-            )
-            spread_of[u] = twice
+            once = work.tile([P, half], BF16, name="once", bufs=2)
+            nc.scalar.copy(out=once[:], in_=coef_t_of.pop(u)[:].rearrange("p g f -> p (g f)"))
+            spread_of[u] = once
 
         def products_gpsimd(u):
             prod = work.tile(unit_shape, F32, name="prod_g", bufs=2)
             nc.gpsimd.tensor_tensor(
-                out=prod[:].rearrange("p g f -> p (g f)"),
-                in0=sine_of.pop(u)[:],
-                in1=spread_of.pop(u)[:].rearrange("p f b -> p (f b)"),
+                out=prod[:].rearrange("p g (f b) -> p (g f) b", b=2),
+                in0=sine_of.pop(u)[:].rearrange("p (f b) -> p f b", b=2),
+                in1=spread_of.pop(u)[:].unsqueeze(2).to_broadcast([P, half, 2]),
                 op=ALU.mult,
             )
             prod_of[u] = prod
@@ -278,12 +276,23 @@ def tile_ka_attention_heads_mod_pa_s_kernel(
             products(u)
             if u % PAIRS == 0 and u > 0:
                 finish(u // PAIRS - 1)
+                emptied.append((u // PAIRS - 1, len(ticks)))
             if u in SPREAD_AFTER:
                 coefficients(SPREAD_AFTER[u])
                 spread(SPREAD_AFTER[u])
             later = [v for v in range(u + 1, UNITS) if not on_gpsimd(v)]
             if not on_gpsimd(u) and len(later) >= 3:
                 coefficients(later[2])
+
+        ticks = []
+        emptied = []
+
+        def tick():
+            ticks.append(0)
+            for j, since in list(emptied):
+                if len(ticks) >= since + ADD_LAG:
+                    emptied.remove((j, since))
+                    shifted(j, nc.gpsimd)
 
         flip(0)
         flip_back(0)
@@ -293,6 +302,7 @@ def tile_ka_attention_heads_mod_pa_s_kernel(
         for w in range(UNITS):
             if w + ROUND_AHEAD < UNITS:
                 rounds(w + ROUND_AHEAD, nc.gpsimd)
+            tick()
             fracs(w)
             sines(w)
             if (w + 4) % PAIRS == 0 and (w + 4) // PAIRS < GROUPS:
@@ -309,7 +319,5 @@ def tile_ka_attention_heads_mod_pa_s_kernel(
             products_gpsimd(u)
         for u in range(made, UNITS):
             product_stage(u)
-            if u == UNITS - 2:
-                for j in range(GROUPS - 1):
-                    shifted(j, nc.gpsimd)
+            tick()
         shifted(GROUPS - 1, nc.vector)

@@ -235,25 +235,37 @@ def tile_ka_attention_heads_mod_pa_s_kernel(
             j, m2 = divmod(u, PAIRS)
             if m2 == 0:
                 summed_of[j] = psum_sum.tile([P, PAIRS, P], F32, name="summed", tag="summed")
+            target = summed_of[j][:, m2, :]
+            pieces = 1
+            if u == UNITS - 1:
+                summed_of[GROUPS] = psum_sum.tile([P, PAIRS, P], F32, name="summed_last", tag="summed")
+                target = summed_of[GROUPS][:, 0, :]
+                pieces = 2
             if on_gpsimd(u):
                 prod = prod_of.pop(u)
             else:
                 prod = work.tile(unit_shape, F32, name="prod")
-                nc.vector.tensor_tensor(
-                    out=prod[:].rearrange("p g (f b) -> p (g f) b", b=2),
-                    in0=sine_of.pop(u)[:].rearrange("p (f b) -> p f b", b=2),
-                    in1=coef_t_of.pop(u)[:].rearrange("p g f -> p (g f)").unsqueeze(2).to_broadcast([P, half, 2]),
-                    op=ALU.mult,
-                )
-            for term in range(2 * TERMS):
-                nc.tensor.matmul(
-                    out=summed_of[j][:, m2, :],
-                    lhsT=prod[:, term, :],
-                    rhs=ident_f32[:],
-                    start=(term == 0),
-                    stop=(term == 2 * TERMS - 1),
-                    is_transpose=True,
-                )
+                sine = sine_of.pop(u)
+                coef_t = coef_t_of.pop(u)
+            count = 2 * TERMS // pieces
+            for piece in range(pieces):
+                terms = slice(piece * count, (piece + 1) * count)
+                if not on_gpsimd(u):
+                    nc.vector.tensor_tensor(
+                        out=prod[:, terms, :].rearrange("p g (f b) -> p (g f) b", b=2),
+                        in0=sine[:, piece * count * P : (piece + 1) * count * P].rearrange("p (f b) -> p f b", b=2),
+                        in1=coef_t[:, terms, :].rearrange("p g f -> p (g f)").unsqueeze(2).to_broadcast([P, count * 64, 2]),
+                        op=ALU.mult,
+                    )
+                for term in range(piece * count, (piece + 1) * count):
+                    nc.tensor.matmul(
+                        out=target,
+                        lhsT=prod[:, term, :],
+                        rhs=ident_f32[:],
+                        start=(term == 0),
+                        stop=(term == 2 * TERMS - 1),
+                        is_transpose=True,
+                    )
 
         def finish(j):
             sums = work.tile([P, PAIRS * P], F32, name="sums", bufs=GROUPS - 1)
@@ -271,6 +283,22 @@ def tile_ka_attention_heads_mod_pa_s_kernel(
             )
             for b in range(2):
                 nc.sync.dma_start(out=out_views[b][:, PAIRS * j : PAIRS * (j + 1), :], in_=result[b:P:2])
+
+        def shifted_end():
+            result = work.tile([P, PAIRS, P], F32, name="result")
+            first = PAIRS * (GROUPS - 1)
+            for source, lo, hi in (
+                (summed_of.pop(GROUPS - 1)[:, 0 : PAIRS - 1, :], 0, PAIRS - 1),
+                (summed_of.pop(GROUPS)[:, 0:1, :], PAIRS - 1, PAIRS),
+            ):
+                nc.vector.tensor_tensor(
+                    out=result[:, lo:hi, :].rearrange("p g f -> p (g f)"),
+                    in0=source.rearrange("p g f -> p (g f)"),
+                    in1=shift_sb[:, first + lo : first + hi, :].rearrange("p g f -> p (g f)"),
+                    op=ALU.add,
+                )
+                for b in range(2):
+                    nc.sync.dma_start(out=out_views[b][:, first + lo : first + hi, :], in_=result[b:P:2, lo:hi, :])
 
         def product_stage(u):
             products(u)
@@ -320,4 +348,4 @@ def tile_ka_attention_heads_mod_pa_s_kernel(
         for u in range(made, UNITS):
             product_stage(u)
             tick()
-        shifted(GROUPS - 1, nc.vector)
+        shifted_end()

@@ -26,6 +26,7 @@ PAIRS = FREQS // 2
 UNITS = GROUPS * PAIRS
 TERMS = 4
 ROUND_AHEAD = 2
+FIRST_ROWS = 13
 GPSIMD_UNITS = (14, 17)
 ADD_LAG = 3
 SPREAD_AFTER = {4: 14, 6: 17}
@@ -118,8 +119,23 @@ def tile_ka_attention_heads_mod_pa_s_kernel(
         nc.scalar.activation(out=turns[:], in_=grid_ps[:], func=ACT.Copy, scale=1.0 / (2.0 * math.pi))
 
         xl = keep.tile([P, ROWS // 2, CHUNKS, QUARTERS, 2], F32, name="xl")
+        accs = []
+
+        def add_bias(cc, rows):
+            count = rows.stop - rows.start
+            nc.vector.tensor_tensor(
+                out=xl[:, rows, cc, :, :],
+                in0=accs[cc][:].rearrange("p d (r b) -> p r d b", b=2)[:, rows],
+                in1=bias_t[:, cc * QUARTERS : (cc + 1) * QUARTERS].unsqueeze(1).unsqueeze(3).to_broadcast([P, count, QUARTERS, 2]),
+                op=ALU.add,
+            )
+
         for cc in range(CHUNKS):
-            acc = psum_setup.tile([P, QUARTERS, ROWS], F32, name="acc", tag="setup")
+            if cc < 3:
+                acc = psum_setup.tile([P, QUARTERS, ROWS], F32, name="acc", tag="setup")
+            else:
+                acc = psum_sum.tile([P, QUARTERS, ROWS], F32, name="acc_more", tag="summed")
+            accs.append(acc)
             for dq in range(QUARTERS):
                 block = cc * QUARTERS + dq
                 nc.tensor.matmul_mx(
@@ -131,12 +147,9 @@ def tile_ka_attention_heads_mod_pa_s_kernel(
                     start=True,
                     stop=True,
                 )
-            nc.vector.tensor_tensor(
-                out=xl[:, :, cc, :, :],
-                in0=acc[:].rearrange("p d (r b) -> p r d b", b=2),
-                in1=bias_t[:, cc * QUARTERS : (cc + 1) * QUARTERS].unsqueeze(1).unsqueeze(3).to_broadcast([P, ROWS // 2, QUARTERS, 2]),
-                op=ALU.add,
-            )
+            add_bias(cc, slice(0, FIRST_ROWS))
+        for cc in range(CHUNKS):
+            add_bias(cc, slice(FIRST_ROWS, ROWS // 2))
         xl_groups = xl[:].rearrange("p r c d b -> p (r c d b)").rearrange("p (j f) -> p j f", j=GROUPS)
         coef_cols = coef_sb[:].rearrange("p a (l m j) -> p a l m j", m=FREQS, j=GROUPS)
         out_views = [out[b].rearrange("h g p (d l) -> (p d) (h g) l", d=QUARTERS) for b in range(2)]

import math
from contextlib import ExitStack

import concourse.mybir as mybir
from concourse.masks import make_identity

F32 = mybir.dt.float32
BF16 = mybir.dt.bfloat16
I32 = mybir.dt.int32
U32 = mybir.dt.uint32
U8 = mybir.dt.uint8
FP8X4 = mybir.dt.float8_e4m3fn_x4
FP4X4 = mybir.dt.float4_e2m1fn_x4
ALU = mybir.AluOpType
ACT = mybir.ActivationFunctionType

P = 128
ROWS = 128
K = 512
GROUPS = 5
FREQS = 8
COLS = GROUPS * K
CHUNKS = 5
QUARTERS = 4
PAIRS = FREQS // 2
UNITS = GROUPS * PAIRS
TERMS = 4
ROUND_AHEAD = 2
FIRST_ROWS = 13
GPSIMD_UNITS = (14, 17)
ADD_LAG = 3
SPREAD_AFTER = {4: 14, 6: 17}

FLOPS = 2 * ROWS * K * COLS


def tile_ka_attention_heads_mod_pa_s_kernel(
    tc, x, lin_w_words, lin_w_scales, lin_b, grid, coef, shift, out
):
    nc = tc.nc
    unit_shape = [P, 2 * TERMS, P]
    half = TERMS * P
    with ExitStack() as stack:
        keep = stack.enter_context(tc.tile_pool(name="keep", bufs=1))
        work = stack.enter_context(tc.tile_pool(name="work", bufs=3))
        psum_setup = stack.enter_context(tc.psum_pool(name="psum_setup", bufs=3))
        psum_coef = stack.enter_context(tc.psum_pool(name="psum_coef", bufs=3))
        psum_sum = stack.enter_context(tc.psum_pool(name="psum_sum", bufs=2))
        stack.enter_context(tc.manual_schedule())

        x_sb = keep.tile([P, K], BF16, name="x_sb")
        nc.sync.dma_start(out=x_sb[:], in_=x.flatten_outer_dims())

        w_words = keep.tile([P, 2 * COLS], U8, name="w_words", align_bytes=64)
        nc.sync.dma_start(out=w_words[:].bitcast(I32), in_=lin_w_words[0].bitcast(I32))
        w_planes = keep.tile([P, COLS], U8, name="w_planes", align_bytes=64)
        nc.vector.memset(w_planes[:].bitcast(I32), 0)
        scale_rows = lin_w_scales[0].rearrange("(q r) n -> r q n", r=4)
        for r in range(4):
            nc.sync.dma_start(
                out=w_planes[r:P:32, :].bitcast(I32), in_=scale_rows[r].bitcast(I32)
            )

        bias_rows = keep.tile([P, P], BF16, name="bias_rows")
        nc.vector.memset(bias_rows[:], 0.0)
        bias_view = lin_b.rearrange("(r c) -> r c", c=P)
        nc.scalar.dma_start(out=bias_rows[0:16, :], in_=bias_view[0:16, :])
        nc.scalar.dma_start(out=bias_rows[16 : COLS // P, :], in_=bias_view[16 : COLS // P, :])
        grid_rows = keep.tile([P, GROUPS * FREQS], BF16, name="grid_rows")
        nc.vector.memset(grid_rows[:], 0.0)
        nc.scalar.dma_start(out=grid_rows[0:1, :], in_=grid.rearrange("(o g) f -> o (g f)", o=1))
        ones = keep.tile([P, P], BF16, name="ones")
        nc.vector.memset(ones[:], 1.0)

        coef_sb = keep.tile([P, 2, P * FREQS * GROUPS], BF16, name="coef_sb")
        coef_halves = coef.rearrange("(a p l) m j -> a p (l m j)", a=2, p=P)
        for a in range(2):
            nc.sync.dma_start(out=coef_sb[:, a, :], in_=coef_halves[a])

        shift_sb = keep.tile([P, UNITS, P], BF16, name="shift_sb")
        shift_view = shift[0].rearrange("h g p (d l) -> (p d) (h g) l", d=QUARTERS)
        for b in range(2):
            nc.sync.dma_start(out=shift_sb[b:P:2], in_=shift_view)

        ident_f32 = keep.tile([P, P], F32, name="ident_f32")
        make_identity(nc, ident_f32[:])
        ident_bf16 = keep.tile([P, P], BF16, name="ident_bf16")
        make_identity(nc, ident_bf16[:])

        warm_in = keep.tile([P, 1], F32, name="warm_in")
        warm_out = keep.tile([P, 1], F32, name="warm_out")
        nc.vector.memset(warm_in[:], 0.0)
        nc.scalar.activation(out=warm_out[:], in_=warm_in[:], func=ACT.Sin)

        x_words = x_sb[:].bitcast(F32)
        x_t = psum_setup.tile([P, 2, ROWS], F32, name="x_t", tag="setup")
        for u in range(2):
            nc.tensor.transpose(x_t[:, u, :], x_words[:, u : K // 2 : 2], ident_f32[:])
        grouped = keep.tile([P, ROWS, 4], BF16, name="grouped", align_bytes=64)
        nc.vector.tensor_copy(
            out=grouped[:].rearrange("p q t -> p (q t)").bitcast(F32).rearrange("p (r b u) -> p r b u", b=2, u=2),
            in_=x_t[:].rearrange("p u (b r) -> p r b u", b=2),
        )
        x_codes = keep.tile([P, ROWS], U32, name="x_codes", align_bytes=64)
        x_scales = keep.tile([P, ROWS], U8, name="x_scales", align_bytes=64)
        nc.vector.quantize_mx(
            out=x_codes[:].bitcast(FP8X4),
            scales=x_scales[:],
            in_=grouped[:].rearrange("p r t -> p (r t)"),
        )

        bias_ps = psum_setup.tile([P, P], BF16, name="bias_ps", tag="setup")
        nc.tensor.transpose(bias_ps[:], bias_rows[:], ident_bf16[:])
        bias_t = keep.tile([P, COLS // P], F32, name="bias_t")
        nc.vector.tensor_copy(out=bias_t[:], in_=bias_ps[:, 0 : COLS // P])
        grid_ps = psum_setup.tile([P, GROUPS * FREQS], F32, name="grid_ps", tag="setup")
        nc.tensor.matmul(out=grid_ps[:], lhsT=ones[:], rhs=grid_rows[:], start=True, stop=True)
        turns = keep.tile([P, GROUPS * FREQS], F32, name="turns")
        nc.scalar.activation(out=turns[:], in_=grid_ps[:], func=ACT.Copy, scale=1.0 / (2.0 * math.pi))

        xl = keep.tile([P, ROWS // 2, CHUNKS, QUARTERS, 2], F32, name="xl")
        accs = []

        def add_bias(cc, rows):
            count = rows.stop - rows.start
            nc.vector.tensor_tensor(
                out=xl[:, rows, cc, :, :],
                in0=accs[cc][:].rearrange("p d (r b) -> p r d b", b=2)[:, rows],
                in1=bias_t[:, cc * QUARTERS : (cc + 1) * QUARTERS].unsqueeze(1).unsqueeze(3).to_broadcast([P, count, QUARTERS, 2]),
                op=ALU.add,
            )

        for cc in range(CHUNKS):
            if cc < 3:
                acc = psum_setup.tile([P, QUARTERS, ROWS], F32, name="acc", tag="setup")
            else:
                acc = psum_sum.tile([P, QUARTERS, ROWS], F32, name="acc_more", tag="summed")
            accs.append(acc)
            for dq in range(QUARTERS):
                block = cc * QUARTERS + dq
                nc.tensor.matmul_mx(
                    out=acc[:, dq, :],
                    lhsT=w_words[:, 2 * P * block : 2 * P * (block + 1)].bitcast(FP4X4),
                    lhsT_scale=w_planes[:, P * block : P * (block + 1)],
                    rhs=x_codes[:].bitcast(FP8X4),
                    rhs_scale=x_scales[:],
                    start=True,
                    stop=True,
                )
            add_bias(cc, slice(0, FIRST_ROWS))
        for cc in range(CHUNKS):
            add_bias(cc, slice(FIRST_ROWS, ROWS // 2))
        xl_groups = xl[:].rearrange("p r c d b -> p (r c d b)").rearrange("p (j f) -> p j f", j=GROUPS)
        coef_cols = coef_sb[:].rearrange("p a (l m j) -> p a l m j", m=FREQS, j=GROUPS)
        out_views = [out[b].rearrange("h g p (d l) -> (p d) (h g) l", d=QUARTERS) for b in range(2)]

        whole_of = {}
        flipped_of = {}
        group_of = {}
        frac_of = {}
        coef_t_of = {}
        sine_of = {}
        summed_of = {}
        spread_of = {}
        prod_of = {}
        sums_of = {}

        def coefficients(u):
            j, m2 = divmod(u, PAIRS)
            coef_t = psum_coef.tile([P, 2 * TERMS, 64], BF16, name="coef_t")
            for e in range(2):
                for a in range(2):
                    nc.tensor.transpose(
                        coef_t[:, e * TERMS + 2 * a : e * TERMS + 2 * a + 2, :].rearrange("p g f -> p (g f)"),
                        coef_cols[:, a, :, 2 * m2 + e, j],
                        ident_bf16[:],
                    )
            coef_t_of[u] = coef_t

        def flip(j):
            flipped_ps = psum_setup.tile([P, TERMS, P], F32, name="flipped_ps", tag="setup")
            for a in range(TERMS):
                nc.tensor.transpose(flipped_ps[:, a, :], xl_groups[:, j, a * P : (a + 1) * P], ident_f32[:])
            flipped = work.tile([P, TERMS, P], F32, name="flipped", bufs=2)
            nc.scalar.copy(out=flipped[:], in_=flipped_ps[:])
            flipped_of[j] = flipped

        def flip_back(j):
            flipped = flipped_of.pop(j)
            group = psum_setup.tile([P, TERMS, P], F32, name="group", tag="setup")
            for a in range(TERMS):
                nc.tensor.transpose(group[:, a, :], flipped[:, a, :], ident_f32[:])
            group_of[j] = group

        def rounds(u, engine):
            j = u // PAIRS
            whole = work.tile([P, 2 * half], I32, name="whole", bufs=4)
            for e in range(2):
                engine.tensor_scalar(
                    out=whole[:, e * half : (e + 1) * half],
                    in0=xl_groups[:, j],
                    scalar1=turns[:, 2 * u + e : 2 * u + e + 1],
                    scalar2=0.0,
                    op0=ALU.mult,
                    op1=ALU.add,
                )
            whole_of[u] = whole

        def fracs(u):
            j = u // PAIRS
            whole = whole_of.pop(u)
            frac = work.tile([P, 2 * half], F32, name="frac")
            for e in range(2):
                nc.vector.scalar_tensor_tensor(
                    out=frac[:, e * half : (e + 1) * half],
                    in0=group_of[j][:].rearrange("p a f -> p (a f)"),
                    scalar=turns[:, 2 * u + e : 2 * u + e + 1],
                    in1=whole[:, e * half : (e + 1) * half],
                    op0=ALU.mult,
                    op1=ALU.subtract,
                )
            frac_of[u] = frac

        def sines(u):
            sine = work.tile([P, 2 * half], F32, name="sine", bufs=10)
            nc.scalar.activation(out=sine[:], in_=frac_of.pop(u)[:], func=ACT.Sin, scale=2.0 * math.pi)
            sine_of[u] = sine

        def on_gpsimd(u):
            return u in GPSIMD_UNITS

        def spread(u):
            once = work.tile([P, half], BF16, name="once", bufs=2)
            nc.scalar.copy(out=once[:], in_=coef_t_of.pop(u)[:].rearrange("p g f -> p (g f)"))
            spread_of[u] = once

        def products_gpsimd(u):
            prod = work.tile(unit_shape, F32, name="prod_g", bufs=2)
            nc.gpsimd.tensor_tensor(
                out=prod[:].rearrange("p g (f b) -> p (g f) b", b=2),
                in0=sine_of.pop(u)[:].rearrange("p (f b) -> p f b", b=2),
                in1=spread_of.pop(u)[:].unsqueeze(2).to_broadcast([P, half, 2]),
                op=ALU.mult,
            )
            prod_of[u] = prod

        def products(u):
            j, m2 = divmod(u, PAIRS)
            if m2 == 0:
                summed_of[j] = psum_sum.tile([P, PAIRS, P], F32, name="summed", tag="summed")
            target = summed_of[j][:, m2, :]
            pieces = 1
            if u == UNITS - 1:
                summed_of[GROUPS] = psum_sum.tile([P, PAIRS, P], F32, name="summed_last", tag="summed")
                target = summed_of[GROUPS][:, 0, :]
                pieces = 2
            if on_gpsimd(u):
                prod = prod_of.pop(u)
            else:
                prod = work.tile(unit_shape, F32, name="prod")
                sine = sine_of.pop(u)
                coef_t = coef_t_of.pop(u)
            count = 2 * TERMS // pieces
            for piece in range(pieces):
                terms = slice(piece * count, (piece + 1) * count)
                if not on_gpsimd(u):
                    nc.vector.tensor_tensor(
                        out=prod[:, terms, :].rearrange("p g (f b) -> p (g f) b", b=2),
                        in0=sine[:, piece * count * P : (piece + 1) * count * P].rearrange("p (f b) -> p f b", b=2),
                        in1=coef_t[:, terms, :].rearrange("p g f -> p (g f)").unsqueeze(2).to_broadcast([P, count * 64, 2]),
                        op=ALU.mult,
                    )
                for term in range(piece * count, (piece + 1) * count):
                    nc.tensor.matmul(
                        out=target,
                        lhsT=prod[:, term, :],
                        rhs=ident_f32[:],
                        start=(term == 0),
                        stop=(term == 2 * TERMS - 1),
                        is_transpose=True,
                    )

        def finish(j):
            sums = work.tile([P, PAIRS * P], F32, name="sums", bufs=GROUPS - 1)
            nc.scalar.copy(out=sums[:], in_=summed_of.pop(j)[:].rearrange("p g f -> p (g f)"))
            sums_of[j] = sums

        def shifted(j, engine):
            sums = sums_of.pop(j)[:] if j in sums_of else summed_of.pop(j)[:].rearrange("p g f -> p (g f)")
            result = work.tile([P, PAIRS, P], F32, name="result")
            engine.tensor_tensor(
                out=result[:].rearrange("p g f -> p (g f)"),
                in0=sums,
                in1=shift_sb[:, PAIRS * j : PAIRS * (j + 1), :].rearrange("p g f -> p (g f)"),
                op=ALU.add,
            )
            for b in range(2):
                nc.sync.dma_start(out=out_views[b][:, PAIRS * j : PAIRS * (j + 1), :], in_=result[b:P:2])

        def shifted_end():
            result = work.tile([P, PAIRS, P], F32, name="result")
            first = PAIRS * (GROUPS - 1)
            for source, lo, hi in (
                (summed_of.pop(GROUPS - 1)[:, 0 : PAIRS - 1, :], 0, PAIRS - 1),
                (summed_of.pop(GROUPS)[:, 0:1, :], PAIRS - 1, PAIRS),
            ):
                nc.vector.tensor_tensor(
                    out=result[:, lo:hi, :].rearrange("p g f -> p (g f)"),
                    in0=source.rearrange("p g f -> p (g f)"),
                    in1=shift_sb[:, first + lo : first + hi, :].rearrange("p g f -> p (g f)"),
                    op=ALU.add,
                )
                for b in range(2):
                    nc.sync.dma_start(out=out_views[b][:, first + lo : first + hi, :], in_=result[b:P:2, lo:hi, :])

        def product_stage(u):
            products(u)
            if u % PAIRS == 0 and u > 0:
                finish(u // PAIRS - 1)
                emptied.append((u // PAIRS - 1, len(ticks)))
            if u in SPREAD_AFTER:
                coefficients(SPREAD_AFTER[u])
                spread(SPREAD_AFTER[u])
            later = [v for v in range(u + 1, UNITS) if not on_gpsimd(v)]
            if not on_gpsimd(u) and len(later) >= 3:
                coefficients(later[2])

        ticks = []
        emptied = []

        def tick():
            ticks.append(0)
            for j, since in list(emptied):
                if len(ticks) >= since + ADD_LAG:
                    emptied.remove((j, since))
                    shifted(j, nc.gpsimd)

        flip(0)
        flip_back(0)
        for u in range(ROUND_AHEAD):
            rounds(u, nc.gpsimd)
        made = 0
        for w in range(UNITS):
            if w + ROUND_AHEAD < UNITS:
                rounds(w + ROUND_AHEAD, nc.gpsimd)
            tick()
            fracs(w)
            sines(w)
            if (w + 4) % PAIRS == 0 and (w + 4) // PAIRS < GROUPS:
                flip((w + 4) // PAIRS)
            if (w + 3) % PAIRS == 0 and (w + 3) // PAIRS < GROUPS:
                flip_back((w + 3) // PAIRS)
            if w == 0:
                for u in range(3):
                    coefficients(u)
            for u in range(made, 2 * w // 3):
                product_stage(u)
            made = max(made, 2 * w // 3)
        for u in GPSIMD_UNITS:
            products_gpsimd(u)
        for u in range(made, UNITS):
            product_stage(u)
            tick()
        shifted_end()
